import numpy as np
import ml_dtypes

BF16 = ml_dtypes.bfloat16


def bf(x):
    return np.asarray(x, np.float32).astype(BF16)


def f32(x):
    return np.asarray(x, np.float32)


def f64(x):
    return np.asarray(x).astype(np.float64)


def striped(idx):
    return np.tile(idx.reshape(-1, 16).T, (8, 1))


C, S, N = 256, 1024, 1024
BASE = 10000.0
TABLE_STD = 0.125


def positional(n, c):
    pos = np.arange(n, dtype=np.float32)[None, :]
    i_even = np.arange(0, c, 2, dtype=np.float32)[:, None]
    inv_freq = np.exp(-(i_even / np.float32(c)) * np.float32(np.log(BASE))).astype(np.float32)
    ang = f64((inv_freq * pos).astype(np.float32))
    return np.stack([np.sin(ang), np.cos(ang)], axis=1).reshape(c, n)


def setup_inputs():
    return {"table": f32(TABLE_STD * np.random.standard_normal((C, S))), "pe": f32(positional(N, C)), "offs": striped(np.random.permutation(np.tile(np.arange(S), 2))[:N])}


def reference(table, pe, offs):
    idx = offs[:16].T.reshape(-1)
    return f64(table)[:, idx] * np.sqrt(C) + f64(pe)

@@ -1,0 +1,39 @@
+import concourse.mybir as mybir
+
+F32 = mybir.dt.float32
+U16 = mybir.dt.uint16
+ADD = mybir.AluOpType.add
+
+P = 128
+CHANNELS = 256
+WORDS = 1024
+TOKENS = 1024
+SCALE = 16.0
+
+
+def tile_tokenembedding_kernel(tc, table, pe, offs, out):
+    nc = tc.nc
+    with (
+        tc.tile_pool(name="held", bufs=1) as held,
+        tc.tile_pool(name="blocks", bufs=2) as blocks,
+    ):
+        offsets = held.tile([P, TOKENS // 16], U16, name="offsets")
+        nc.sync.dma_start(offsets[:], offs)
+
+        for block in range(CHANNELS // P):
+            rows = slice(block * P, (block + 1) * P)
+
+            window = blocks.tile([P, WORDS], F32, name="window")
+            nc.sync.dma_start(window[:], table[rows, :])
+            place = blocks.tile([P, TOKENS], F32, name="place")
+            nc.sync.dma_start(place[:], pe[rows, :])
+
+            place_small = blocks.tile([P, TOKENS], F32, name="place_small")
+            nc.scalar.mul(place_small[:], place[:], 1.0 / SCALE)
+
+            summed = blocks.tile([P, TOKENS], F32, name="summed")
+            nc.vector.tensor_tensor(summed[:], window[:].indirect(offsets[:]), place_small[:], ADD)
+
+            result = blocks.tile([P, TOKENS], F32, name="result")
+            nc.scalar.mul(result[:], summed[:], SCALE)
+            nc.sync.dma_start(out[rows, :], result[:])

@@ -10,30 +10,53 @@ WORDS = 1024
 TOKENS = 1024
 SCALE = 16.0
 
+BLOCKS = CHANNELS // P
+PIECE = 256
+PIECES = TOKENS // PIECE
+STEPS = BLOCKS * PIECES
+AHEAD = 2
+
 
 def tile_tokenembedding_kernel(tc, table, pe, offs, out):
     nc = tc.nc
-    with (
-        tc.tile_pool(name="held", bufs=1) as held,
-        tc.tile_pool(name="blocks", bufs=2) as blocks,
-    ):
+    with tc.tile_pool(name="held", bufs=1) as held:
         offsets = held.tile([P, TOKENS // 16], U16, name="offsets")
         nc.sync.dma_start(offsets[:], offs)
 
-        for block in range(CHANNELS // P):
+        windows = []
+        places = []
+        for block in range(BLOCKS):
+            rows = slice(block * P, (block + 1) * P)
+            window = held.tile([P, WORDS], F32, name=f"window{block}")
+            windows.append(window)
+            for piece in range(PIECES):
+                place = held.tile([P, PIECE], F32, name=f"place{block}_{piece}")
+                places.append(place)
+                nc.sync.dma_start(place[:], pe[rows, piece * PIECE : (piece + 1) * PIECE])
+                if piece == 0:
+                    nc.sync.dma_start(window[:], table[rows, :])
+
+        shrunk = []
+        for step in range(AHEAD):
+            small = held.tile([P, PIECE], F32, name=f"small{step}")
+            shrunk.append(small)
+            nc.scalar.mul(small[:], places[step][:], 1.0 / SCALE)
+
+        for step in range(STEPS):
+            block, piece = divmod(step, PIECES)
             rows = slice(block * P, (block + 1) * P)
 
-            window = blocks.tile([P, WORDS], F32, name="window")
-            nc.sync.dma_start(window[:], table[rows, :])
-            place = blocks.tile([P, TOKENS], F32, name="place")
-            nc.sync.dma_start(place[:], pe[rows, :])
+            if step + AHEAD < STEPS:
+                small = held.tile([P, PIECE], F32, name=f"small{step + AHEAD}")
+                shrunk.append(small)
+                nc.scalar.mul(small[:], places[step + AHEAD][:], 1.0 / SCALE)
 
-            place_small = blocks.tile([P, TOKENS], F32, name="place_small")
-            nc.scalar.mul(place_small[:], place[:], 1.0 / SCALE)
+            piece_offsets = offsets[:, piece * PIECE // 16 : (piece + 1) * PIECE // 16]
+            summed = held.tile([P, PIECE], F32, name=f"summed{step}")
+            nc.vector.tensor_tensor(
+                summed[:], windows[block][:].indirect(piece_offsets), shrunk[step][:], ADD
+            )
 
-            summed = blocks.tile([P, TOKENS], F32, name="summed")
-            nc.vector.tensor_tensor(summed[:], window[:].indirect(offsets[:]), place_small[:], ADD)
-
-            result = blocks.tile([P, TOKENS], F32, name="result")
+            result = held.tile([P, PIECE], F32, name=f"result{step}")
             nc.scalar.mul(result[:], summed[:], SCALE)
-            nc.sync.dma_start(out[rows, :], result[:])
+            nc.sync.dma_start(out[rows, piece * PIECE : (piece + 1) * PIECE], result[:])

@@ -27,20 +27,19 @@ def tile_tokenembedding_kernel(tc, table, pe, offs, out):
         places = []
         for block in range(BLOCKS):
             rows = slice(block * P, (block + 1) * P)
+            place = held.tile([P, TOKENS], F32, name=f"place{block}")
+            nc.sync.dma_start(place[:], pe[rows, :])
             window = held.tile([P, WORDS], F32, name=f"window{block}")
+            nc.sync.dma_start(window[:], table[rows, :])
             windows.append(window)
             for piece in range(PIECES):
-                place = held.tile([P, PIECE], F32, name=f"place{block}_{piece}")
-                places.append(place)
-                nc.sync.dma_start(place[:], pe[rows, piece * PIECE : (piece + 1) * PIECE])
-                if piece == 0:
-                    nc.sync.dma_start(window[:], table[rows, :])
+                places.append(place[:, piece * PIECE : (piece + 1) * PIECE])
 
         shrunk = []
         for step in range(AHEAD):
             small = held.tile([P, PIECE], F32, name=f"small{step}")
             shrunk.append(small)
-            nc.scalar.mul(small[:], places[step][:], 1.0 / SCALE)
+            nc.scalar.mul(small[:], places[step], 1.0 / SCALE)
 
         for step in range(STEPS):
             block, piece = divmod(step, PIECES)
@@ -49,7 +48,7 @@ def tile_tokenembedding_kernel(tc, table, pe, offs, out):
             if step + AHEAD < STEPS:
                 small = held.tile([P, PIECE], F32, name=f"small{step + AHEAD}")
                 shrunk.append(small)
-                nc.scalar.mul(small[:], places[step + AHEAD][:], 1.0 / SCALE)
+                nc.scalar.mul(small[:], places[step + AHEAD], 1.0 / SCALE)
 
             piece_offsets = offsets[:, piece * PIECE // 16 : (piece + 1) * PIECE // 16]
             summed = held.tile([P, PIECE], F32, name=f"summed{step}")

@@ -11,14 +11,20 @@ TOKENS = 1024
 SCALE = 16.0
 
 BLOCKS = CHANNELS // P
-PIECE = 256
-PIECES = TOKENS // PIECE
-STEPS = BLOCKS * PIECES
+HALF = TOKENS // 2
 AHEAD = 2
+
+
+def cut_steps():
+    steps = [(block, first, HALF) for block in range(BLOCKS) for first in (0, HALF)]
+    block, first, tokens = steps[-1]
+    quarter = tokens // 2
+    return steps[:-1] + [(block, first, quarter), (block, first + quarter, quarter)]
 
 
 def tile_tokenembedding_kernel(tc, table, pe, offs, out):
     nc = tc.nc
+    steps = cut_steps()
     with tc.tile_pool(name="held", bufs=1) as held:
         offsets = held.tile([P, TOKENS // 16], U16, name="offsets")
         nc.sync.dma_start(offsets[:], offs)
@@ -29,33 +35,32 @@ def tile_tokenembedding_kernel(tc, table, pe, offs, out):
             rows = slice(block * P, (block + 1) * P)
             place = held.tile([P, TOKENS], F32, name=f"place{block}")
             nc.sync.dma_start(place[:], pe[rows, :])
+            places.append(place)
             window = held.tile([P, WORDS], F32, name=f"window{block}")
             nc.sync.dma_start(window[:], table[rows, :])
             windows.append(window)
-            for piece in range(PIECES):
-                places.append(place[:, piece * PIECE : (piece + 1) * PIECE])
 
         shrunk = []
-        for step in range(AHEAD):
-            small = held.tile([P, PIECE], F32, name=f"small{step}")
+
+        def shrink(step):
+            block, first, tokens = steps[step]
+            small = held.tile([P, tokens], F32, name=f"small{step}")
+            nc.scalar.mul(small[:], places[block][:, first : first + tokens], 1.0 / SCALE)
             shrunk.append(small)
-            nc.scalar.mul(small[:], places[step], 1.0 / SCALE)
 
-        for step in range(STEPS):
-            block, piece = divmod(step, PIECES)
-            rows = slice(block * P, (block + 1) * P)
+        for step in range(AHEAD):
+            shrink(step)
 
-            if step + AHEAD < STEPS:
-                small = held.tile([P, PIECE], F32, name=f"small{step + AHEAD}")
-                shrunk.append(small)
-                nc.scalar.mul(small[:], places[step + AHEAD], 1.0 / SCALE)
+        for step, (block, first, tokens) in enumerate(steps):
+            if step + AHEAD < len(steps):
+                shrink(step + AHEAD)
 
-            piece_offsets = offsets[:, piece * PIECE // 16 : (piece + 1) * PIECE // 16]
-            summed = held.tile([P, PIECE], F32, name=f"summed{step}")
+            step_offsets = offsets[:, first // 16 : (first + tokens) // 16]
+            summed = held.tile([P, tokens], F32, name=f"summed{step}")
             nc.vector.tensor_tensor(
-                summed[:], windows[block][:].indirect(piece_offsets), shrunk[step][:], ADD
+                summed[:], windows[block][:].indirect(step_offsets), shrunk[step][:], ADD
             )
 
-            result = held.tile([P, PIECE], F32, name=f"result{step}")
+            result = held.tile([P, tokens], F32, name=f"result{step}")
             nc.scalar.mul(result[:], summed[:], SCALE)
-            nc.sync.dma_start(out[rows, piece * PIECE : (piece + 1) * PIECE], result[:])
+            nc.sync.dma_start(out[block * P : (block + 1) * P, first : first + tokens], result[:])

@@ -12,55 +12,55 @@ SCALE = 16.0
 
 BLOCKS = CHANNELS // P
 HALF = TOKENS // 2
-AHEAD = 2
+QUARTER = TOKENS // 4
 
 
 def cut_steps():
     steps = [(block, first, HALF) for block in range(BLOCKS) for first in (0, HALF)]
-    block, first, tokens = steps[-1]
-    quarter = tokens // 2
-    return steps[:-1] + [(block, first, quarter), (block, first + quarter, quarter)]
+    cut = []
+    for number, (block, first, tokens) in enumerate(steps):
+        if number in (0, len(steps) - 1):
+            cut += [(block, first, QUARTER), (block, first + QUARTER, QUARTER)]
+        else:
+            cut.append((block, first, tokens))
+    return cut
 
 
 def tile_tokenembedding_kernel(tc, table, pe, offs, out):
     nc = tc.nc
-    steps = cut_steps()
     with tc.tile_pool(name="held", bufs=1) as held:
         offsets = held.tile([P, TOKENS // 16], U16, name="offsets")
-        nc.sync.dma_start(offsets[:], offs)
+        words = [held.tile([P, WORDS], F32, name=f"word{block}") for block in range(BLOCKS)]
+        places = [held.tile([P, TOKENS], F32, name=f"place{block}") for block in range(BLOCKS)]
+        windows = [held.tile([P, WORDS], F32, name=f"window{block}") for block in range(BLOCKS)]
 
-        windows = []
-        places = []
-        for block in range(BLOCKS):
-            rows = slice(block * P, (block + 1) * P)
-            place = held.tile([P, TOKENS], F32, name=f"place{block}")
-            nc.sync.dma_start(place[:], pe[rows, :])
-            places.append(place)
-            window = held.tile([P, WORDS], F32, name=f"window{block}")
-            nc.sync.dma_start(window[:], table[rows, :])
-            windows.append(window)
-
-        shrunk = []
-
-        def shrink(step):
-            block, first, tokens = steps[step]
-            small = held.tile([P, tokens], F32, name=f"small{step}")
-            nc.scalar.mul(small[:], places[block][:, first : first + tokens], 1.0 / SCALE)
-            shrunk.append(small)
-
-        for step in range(AHEAD):
-            shrink(step)
-
-        for step, (block, first, tokens) in enumerate(steps):
-            if step + AHEAD < len(steps):
-                shrink(step + AHEAD)
-
-            step_offsets = offsets[:, first // 16 : (first + tokens) // 16]
-            summed = held.tile([P, tokens], F32, name=f"summed{step}")
-            nc.vector.tensor_tensor(
-                summed[:], windows[block][:].indirect(step_offsets), shrunk[step][:], ADD
+        def load(tile, source, block, first, columns):
+            nc.sync.dma_start(
+                tile[:, first : first + columns],
+                source[block * P : (block + 1) * P, first : first + columns],
             )
 
+        load(words[0], table, 0, 0, HALF)
+        load(words[0], table, 0, HALF, HALF)
+        nc.sync.dma_start(offsets[:], offs)
+        load(places[0], pe, 0, 0, QUARTER)
+        load(places[0], pe, 0, QUARTER, TOKENS - QUARTER)
+        load(words[1], table, 1, 0, HALF)
+        load(words[1], table, 1, HALF, HALF)
+        load(places[1], pe, 1, 0, TOKENS)
+
+        nc.scalar.mul(windows[0][:, :HALF], words[0][:, :HALF], SCALE)
+        nc.vector.tensor_scalar_mul(windows[0][:, HALF:], words[0][:, HALF:], SCALE)
+        nc.scalar.mul(windows[1][:, :HALF], words[1][:, :HALF], SCALE)
+        nc.scalar.mul(windows[1][:, HALF:], words[1][:, HALF:], SCALE)
+
+        for step, (block, first, tokens) in enumerate(cut_steps()):
+            step_offsets = offsets[:, first // 16 : (first + tokens) // 16]
             result = held.tile([P, tokens], F32, name=f"result{step}")
-            nc.scalar.mul(result[:], summed[:], SCALE)
+            nc.vector.tensor_tensor(
+                result[:],
+                windows[block][:].indirect(step_offsets),
+                places[block][:, first : first + tokens],
+                ADD,
+            )
             nc.sync.dma_start(out[block * P : (block + 1) * P, first : first + tokens], result[:])

@@ -44,10 +44,12 @@ def tile_tokenembedding_kernel(tc, table, pe, offs, out):
         load(words[0], table, 0, HALF, HALF)
         nc.sync.dma_start(offsets[:], offs)
         load(places[0], pe, 0, 0, QUARTER)
-        load(places[0], pe, 0, QUARTER, TOKENS - QUARTER)
+        load(places[0], pe, 0, QUARTER, QUARTER)
         load(words[1], table, 1, 0, HALF)
+        load(places[0], pe, 0, HALF, HALF)
         load(words[1], table, 1, HALF, HALF)
-        load(places[1], pe, 1, 0, TOKENS)
+        load(places[1], pe, 1, 0, HALF)
+        load(places[1], pe, 1, HALF, HALF)
 
         nc.scalar.mul(windows[0][:, :HALF], words[0][:, :HALF], SCALE)
         nc.vector.tensor_scalar_mul(windows[0][:, HALF:], words[0][:, HALF:], SCALE)

@@ -41,28 +41,37 @@ def tile_tokenembedding_kernel(tc, table, pe, offs, out):
             )
 
         load(words[0], table, 0, 0, HALF)
-        load(words[0], table, 0, HALF, HALF)
+        load(words[0], table, 0, HALF, QUARTER)
+        load(words[0], table, 0, HALF + QUARTER, QUARTER)
         nc.sync.dma_start(offsets[:], offs)
         load(places[0], pe, 0, 0, QUARTER)
         load(places[0], pe, 0, QUARTER, QUARTER)
         load(words[1], table, 1, 0, HALF)
         load(places[0], pe, 0, HALF, HALF)
-        load(words[1], table, 1, HALF, HALF)
+        load(words[1], table, 1, HALF, QUARTER)
+        load(words[1], table, 1, HALF + QUARTER, QUARTER)
         load(places[1], pe, 1, 0, HALF)
         load(places[1], pe, 1, HALF, HALF)
 
-        nc.scalar.mul(windows[0][:, :HALF], words[0][:, :HALF], SCALE)
-        nc.vector.tensor_scalar_mul(windows[0][:, HALF:], words[0][:, HALF:], SCALE)
-        nc.scalar.mul(windows[1][:, :HALF], words[1][:, :HALF], SCALE)
-        nc.scalar.mul(windows[1][:, HALF:], words[1][:, HALF:], SCALE)
+        pieces = (slice(0, HALF), slice(HALF, HALF + QUARTER), slice(HALF + QUARTER, WORDS))
+        nc.scalar.mul(windows[0][:, pieces[0]], words[0][:, pieces[0]], SCALE)
+        nc.vector.tensor_scalar_mul(windows[0][:, pieces[1]], words[0][:, pieces[1]], SCALE)
+        nc.vector.tensor_scalar_mul(windows[0][:, pieces[2]], words[0][:, pieces[2]], SCALE)
+        for piece in pieces:
+            nc.scalar.mul(windows[1][:, piece], words[1][:, piece], SCALE)
 
-        for step, (block, first, tokens) in enumerate(cut_steps()):
+        results = [held.tile([P, TOKENS], F32, name=f"result{block}") for block in range(BLOCKS)]
+        for block, first, tokens in cut_steps():
             step_offsets = offsets[:, first // 16 : (first + tokens) // 16]
-            result = held.tile([P, tokens], F32, name=f"result{step}")
             nc.vector.tensor_tensor(
-                result[:],
+                results[block][:, first : first + tokens],
                 windows[block][:].indirect(step_offsets),
                 places[block][:, first : first + tokens],
                 ADD,
             )
-            nc.sync.dma_start(out[block * P : (block + 1) * P, first : first + tokens], result[:])
+            if block == 0 and first + tokens == TOKENS:
+                nc.sync.dma_start(out[0:P, :], results[0][:])
+            if block == 1:
+                nc.sync.dma_start(
+                    out[P : 2 * P, first : first + tokens], results[1][:, first : first + tokens]
+                )

@@ -54,9 +54,8 @@ def tile_tokenembedding_kernel(tc, table, pe, offs, out):
         load(places[1], pe, 1, HALF, HALF)
 
         pieces = (slice(0, HALF), slice(HALF, HALF + QUARTER), slice(HALF + QUARTER, WORDS))
-        nc.scalar.mul(windows[0][:, pieces[0]], words[0][:, pieces[0]], SCALE)
-        nc.vector.tensor_scalar_mul(windows[0][:, pieces[1]], words[0][:, pieces[1]], SCALE)
-        nc.vector.tensor_scalar_mul(windows[0][:, pieces[2]], words[0][:, pieces[2]], SCALE)
+        for piece in pieces:
+            nc.vector.tensor_scalar_mul(windows[0][:, piece], words[0][:, piece], SCALE)
         for piece in pieces:
             nc.scalar.mul(windows[1][:, piece], words[1][:, piece], SCALE)
 

@@ -13,17 +13,19 @@ SCALE = 16.0
 BLOCKS = CHANNELS // P
 HALF = TOKENS // 2
 QUARTER = TOKENS // 4
+FIRST = TOKENS // 8
+REST = (TOKENS - FIRST) // 2
 
 
 def cut_steps():
-    steps = [(block, first, HALF) for block in range(BLOCKS) for first in (0, HALF)]
-    cut = []
-    for number, (block, first, tokens) in enumerate(steps):
-        if number in (0, len(steps) - 1):
-            cut += [(block, first, QUARTER), (block, first + QUARTER, QUARTER)]
-        else:
-            cut.append((block, first, tokens))
-    return cut
+    cuts = ((FIRST, REST, REST), (HALF, QUARTER, QUARTER))
+    steps = []
+    for block, cut in enumerate(cuts):
+        first = 0
+        for tokens in cut:
+            steps.append((block, first, tokens))
+            first += tokens
+    return steps
 
 
 def tile_tokenembedding_kernel(tc, table, pe, offs, out):
@@ -44,10 +46,10 @@ def tile_tokenembedding_kernel(tc, table, pe, offs, out):
         load(words[0], table, 0, HALF, QUARTER)
         load(words[0], table, 0, HALF + QUARTER, QUARTER)
         nc.sync.dma_start(offsets[:], offs)
-        load(places[0], pe, 0, 0, QUARTER)
-        load(places[0], pe, 0, QUARTER, QUARTER)
+        load(places[0], pe, 0, 0, FIRST)
+        load(places[0], pe, 0, FIRST, REST)
         load(words[1], table, 1, 0, HALF)
-        load(places[0], pe, 0, HALF, HALF)
+        load(places[0], pe, 0, FIRST + REST, REST)
         load(words[1], table, 1, HALF, QUARTER)
         load(words[1], table, 1, HALF + QUARTER, QUARTER)
         load(places[1], pe, 1, 0, HALF)

@@ -17,17 +17,6 @@ FIRST = TOKENS // 8
 REST = (TOKENS - FIRST) // 2
 
 
-def cut_steps():
-    cuts = ((FIRST, REST, REST), (HALF, QUARTER, QUARTER))
-    steps = []
-    for block, cut in enumerate(cuts):
-        first = 0
-        for tokens in cut:
-            steps.append((block, first, tokens))
-            first += tokens
-    return steps
-
-
 def tile_tokenembedding_kernel(tc, table, pe, offs, out):
     nc = tc.nc
     with tc.tile_pool(name="held", bufs=1) as held:
@@ -35,6 +24,9 @@ def tile_tokenembedding_kernel(tc, table, pe, offs, out):
         words = [held.tile([P, WORDS], F32, name=f"word{block}") for block in range(BLOCKS)]
         places = [held.tile([P, TOKENS], F32, name=f"place{block}") for block in range(BLOCKS)]
         windows = [held.tile([P, WORDS], F32, name=f"window{block}") for block in range(BLOCKS)]
+        results = [held.tile([P, TOKENS], F32, name=f"result{block}") for block in range(BLOCKS)]
+        small_place = held.tile([P, QUARTER], F32, name="small_place")
+        small_sum = held.tile([P, QUARTER], F32, name="small_sum")
 
         def load(tile, source, block, first, columns):
             nc.sync.dma_start(
@@ -50,29 +42,30 @@ def tile_tokenembedding_kernel(tc, table, pe, offs, out):
         load(places[0], pe, 0, FIRST, REST)
         load(words[1], table, 1, 0, HALF)
         load(places[0], pe, 0, FIRST + REST, REST)
-        load(words[1], table, 1, HALF, QUARTER)
-        load(words[1], table, 1, HALF + QUARTER, QUARTER)
-        load(places[1], pe, 1, 0, HALF)
-        load(places[1], pe, 1, HALF, HALF)
+        load(places[1], pe, 1, 0, QUARTER)
+        load(words[1], table, 1, HALF, HALF)
+        load(places[1], pe, 1, QUARTER, TOKENS - QUARTER)
 
         pieces = (slice(0, HALF), slice(HALF, HALF + QUARTER), slice(HALF + QUARTER, WORDS))
         for piece in pieces:
             nc.vector.tensor_scalar_mul(windows[0][:, piece], words[0][:, piece], SCALE)
-        for piece in pieces:
-            nc.scalar.mul(windows[1][:, piece], words[1][:, piece], SCALE)
+        nc.scalar.mul(windows[1][:, 0:HALF], words[1][:, 0:HALF], SCALE)
+        nc.scalar.mul(small_place[:], places[1][:, 0:QUARTER], 1.0 / SCALE)
+        nc.scalar.mul(windows[1][:, HALF:WORDS], words[1][:, HALF:WORDS], SCALE)
 
-        results = [held.tile([P, TOKENS], F32, name=f"result{block}") for block in range(BLOCKS)]
-        for block, first, tokens in cut_steps():
+        def look_up(summed, window, place, first, tokens):
             step_offsets = offsets[:, first // 16 : (first + tokens) // 16]
-            nc.vector.tensor_tensor(
-                results[block][:, first : first + tokens],
-                windows[block][:].indirect(step_offsets),
-                places[block][:, first : first + tokens],
-                ADD,
-            )
-            if block == 0 and first + tokens == TOKENS:
-                nc.sync.dma_start(out[0:P, :], results[0][:])
-            if block == 1:
-                nc.sync.dma_start(
-                    out[P : 2 * P, first : first + tokens], results[1][:, first : first + tokens]
-                )
+            nc.vector.tensor_tensor(summed, window[:].indirect(step_offsets), place, ADD)
+
+        for first, tokens in ((0, FIRST), (FIRST, REST), (FIRST + REST, REST)):
+            step = slice(first, first + tokens)
+            look_up(results[0][:, step], windows[0], places[0][:, step], first, tokens)
+        nc.sync.dma_start(out[0:P, :], results[0][:])
+
+        look_up(small_sum[:], words[1], small_place[:], 0, QUARTER)
+        nc.scalar.mul(results[1][:, 0:QUARTER], small_sum[:], SCALE)
+        nc.sync.dma_start(out[P : 2 * P, 0:QUARTER], results[1][:, 0:QUARTER])
+        for first, tokens in ((QUARTER, HALF), (QUARTER + HALF, QUARTER)):
+            step = slice(first, first + tokens)
+            look_up(results[1][:, step], windows[1], places[1][:, step], first, tokens)
+            nc.sync.dma_start(out[P : 2 * P, step], results[1][:, step])

@@ -44,7 +44,8 @@ def tile_tokenembedding_kernel(tc, table, pe, offs, out):
         load(places[0], pe, 0, FIRST + REST, REST)
         load(places[1], pe, 1, 0, QUARTER)
         load(words[1], table, 1, HALF, HALF)
-        load(places[1], pe, 1, QUARTER, TOKENS - QUARTER)
+        load(places[1], pe, 1, QUARTER, HALF)
+        load(places[1], pe, 1, QUARTER + HALF, QUARTER)
 
         pieces = (slice(0, HALF), slice(HALF, HALF + QUARTER), slice(HALF + QUARTER, WORDS))
         for piece in pieces:

import concourse.mybir as mybir

F32 = mybir.dt.float32
U16 = mybir.dt.uint16
ADD = mybir.AluOpType.add

P = 128
CHANNELS = 256
WORDS = 1024
TOKENS = 1024
SCALE = 16.0

BLOCKS = CHANNELS // P
HALF = TOKENS // 2
QUARTER = TOKENS // 4
FIRST = TOKENS // 8
REST = (TOKENS - FIRST) // 2


def tile_tokenembedding_kernel(tc, table, pe, offs, out):
    nc = tc.nc
    with tc.tile_pool(name="held", bufs=1) as held:
        offsets = held.tile([P, TOKENS // 16], U16, name="offsets")
        words = [held.tile([P, WORDS], F32, name=f"word{block}") for block in range(BLOCKS)]
        places = [held.tile([P, TOKENS], F32, name=f"place{block}") for block in range(BLOCKS)]
        windows = [held.tile([P, WORDS], F32, name=f"window{block}") for block in range(BLOCKS)]
        results = [held.tile([P, TOKENS], F32, name=f"result{block}") for block in range(BLOCKS)]
        small_place = held.tile([P, QUARTER], F32, name="small_place")
        small_sum = held.tile([P, QUARTER], F32, name="small_sum")

        def load(tile, source, block, first, columns):
            nc.sync.dma_start(
                tile[:, first : first + columns],
                source[block * P : (block + 1) * P, first : first + columns],
            )

        load(words[0], table, 0, 0, HALF)
        load(words[0], table, 0, HALF, QUARTER)
        load(words[0], table, 0, HALF + QUARTER, QUARTER)
        nc.sync.dma_start(offsets[:], offs)
        load(places[0], pe, 0, 0, FIRST)
        load(places[0], pe, 0, FIRST, REST)
        load(words[1], table, 1, 0, HALF)
        load(places[0], pe, 0, FIRST + REST, REST)
        load(places[1], pe, 1, 0, QUARTER)
        load(words[1], table, 1, HALF, HALF)
        load(places[1], pe, 1, QUARTER, HALF)
        load(places[1], pe, 1, QUARTER + HALF, QUARTER)

        pieces = (slice(0, HALF), slice(HALF, HALF + QUARTER), slice(HALF + QUARTER, WORDS))
        for piece in pieces:
            nc.vector.tensor_scalar_mul(windows[0][:, piece], words[0][:, piece], SCALE)
        nc.scalar.mul(windows[1][:, 0:HALF], words[1][:, 0:HALF], SCALE)
        nc.scalar.mul(small_place[:], places[1][:, 0:QUARTER], 1.0 / SCALE)
        nc.scalar.mul(windows[1][:, HALF:WORDS], words[1][:, HALF:WORDS], SCALE)

        def look_up(summed, window, place, first, tokens):
            step_offsets = offsets[:, first // 16 : (first + tokens) // 16]
            nc.vector.tensor_tensor(summed, window[:].indirect(step_offsets), place, ADD)

        for first, tokens in ((0, FIRST), (FIRST, REST), (FIRST + REST, REST)):
            step = slice(first, first + tokens)
            look_up(results[0][:, step], windows[0], places[0][:, step], first, tokens)
        nc.sync.dma_start(out[0:P, :], results[0][:])

        look_up(small_sum[:], words[1], small_place[:], 0, QUARTER)
        nc.scalar.mul(results[1][:, 0:QUARTER], small_sum[:], SCALE)
        nc.sync.dma_start(out[P : 2 * P, 0:QUARTER], results[1][:, 0:QUARTER])
        for first, tokens in ((QUARTER, HALF), (QUARTER + HALF, QUARTER)):
            step = slice(first, first + tokens)
            look_up(results[1][:, step], windows[1], places[1][:, step], first, tokens)
            nc.sync.dma_start(out[P : 2 * P, step], results[1][:, step])
